import numpy as np
import ml_dtypes


def mxq(x, axis, fmt="e4m3"):
    dtype, down = {"e4m3": (ml_dtypes.float8_e4m3fn, 7), "e5m2": (ml_dtypes.float8_e5m2, 14)}[fmt]
    v = np.moveaxis(np.asarray(x, np.float32).astype(ml_dtypes.bfloat16).astype(np.float64), axis, -1)
    blocks = v.reshape(v.shape[:-1] + (-1, 32))
    amax = np.abs(blocks).max(-1, keepdims=True)
    byte = np.maximum(np.where(amax > 0, np.frexp(amax)[1] - 1 + 127, 0) - down, 1)
    scale = np.exp2(byte - 127.0)
    codes = (blocks / scale).astype(np.float32).astype(dtype).astype(np.float64)
    return np.moveaxis((codes * scale).reshape(v.shape), -1, axis)


WIDE = False


def mx_kscale(k):
    if not WIDE:
        return np.ones(k)
    levels = np.array([18, -18])
    if k % 512:
        return np.exp2(np.random.permutation(np.resize(levels, k // 32))).repeat(32)
    a = np.empty((k // 512, 16))
    for p in range(k // 512):
        a[p, :8] = np.random.permutation(np.resize(levels, 8))
        for g in range(8):
            far = levels[np.abs(levels - a[p, g]) >= 10]
            a[p, g + 8] = far[np.random.randint(len(far))]
    return np.exp2(a.ravel()).repeat(32)


BF16 = ml_dtypes.bfloat16


def bf(x):
    return np.asarray(x, np.float32).astype(BF16)


def f64(x):
    return np.asarray(x).astype(np.float64)


B, S, D, H, DH, DL, DR = 2, 512, 2048, 16, 128, 512, 64
ROPE_BASE = 10000.0
T = B * S
J = H * (DH + DR)


def rope_tables():
    inv_freq = 1.0 / ROPE_BASE ** (np.arange(0, DR, 2) / DR)
    freqs = np.arange(S)[:, None] * inv_freq[None, :]
    emb = np.concatenate([freqs, freqs], axis=-1)
    return np.cos(emb), np.sin(emb)


def rotate_half(u):
    u1, u2 = np.split(u, 2, axis=-1)
    return np.concatenate([-u2, u1], axis=-1)


def rotate_half_back(u):
    u1, u2 = np.split(u, 2, axis=-1)
    return np.concatenate([u2, -u1], axis=-1)


def setup_inputs():
    s = mx_kscale(T)
    v = mx_kscale(DL)
    u = np.array(mx_kscale(J)).reshape(H, DH + DR)
    u[:, DH + DR // 2:] = u[:, DH:DH + DR // 2]
    x0 = bf(np.random.standard_normal((B, S, D)))
    wd0 = bf(np.random.standard_normal((D, DL)) / np.sqrt(D))
    wu0 = bf(np.random.standard_normal((DL, J)) / np.sqrt(DL))
    g = bf(np.random.standard_normal((B, S, H, DH + DR)) * np.exp2(np.random.randint(-6, 1, (B, S, 1, 1))) / s.reshape(B, S, 1, 1) * u)
    cos, sin = rope_tables()
    return {"x": bf(f64(x0) * s.reshape(B, S, 1)),
            "W_q_down": bf(f64(wd0) / v),
            "W_q_up": bf(f64(wu0) * v[:, None] / u.reshape(J)),
            "rope_cos": np.asarray(cos, np.float32),
            "rope_sin": np.asarray(sin, np.float32),
            "grad_out": g}


def reference(x, W_q_down, W_q_up, rope_cos, rope_sin, grad_out):
    g = f64(grad_out)
    cos, sin = f64(rope_cos)[None, :, None, :], f64(rope_sin)[None, :, None, :]
    gr = g[..., DH:]
    dr = gr * cos + rotate_half_back(gr * sin)
    dz2 = np.concatenate([g[..., :DH], dr], axis=-1).reshape(T, J)
    dz1 = mxq(dz2, 1, "e5m2") @ mxq(f64(W_q_up), 1, "e4m3").T
    dx = mxq(dz1, 1, "e5m2") @ mxq(f64(W_q_down), 1, "e4m3").T
    dw = mxq(f64(x).reshape(T, D), 0, "e4m3").T @ mxq(dz1, 0, "e5m2")
    return dx.reshape(B, S, D), dw

@@ -1,0 +1,421 @@
+from contextlib import ExitStack
+
+import concourse.mybir as mybir
+from concourse.masks import make_identity
+
+B, S, D, H, DH, DL, DR = 2, 512, 2048, 16, 128, 512, 64
+T = B * S
+J = H * (DH + DR)
+FLOPS = 2 * T * J * DL + 2 * T * DL * D + 2 * D * T * DL
+
+F32 = mybir.dt.float32
+BF16 = mybir.dt.bfloat16
+U32 = mybir.dt.uint32
+U8 = mybir.dt.uint8
+E4M3 = mybir.dt.float8_e4m3fn_x4
+E5M2 = mybir.dt.float8_e5m2_x4
+MULT = mybir.AluOpType.mult
+ADD = mybir.AluOpType.add
+SUB = mybir.AluOpType.subtract
+
+P = 128
+PASSES = J // 512
+TILES = T // P
+GTILES = S // P
+HF = DH + DR
+
+
+def tile_multilatentattention_pb_v_kernel(tc, x, wd, wu, rope_cos, rope_sin, g, out_0, out_1):
+    nc = tc.nc
+
+    g_view = g.rearrange("b (p j) h f -> b p j (h f)", j=4)
+    x_view = x.rearrange("b (p j) d -> b p j d", j=4)
+    wu_view = wu.rearrange("(p u e) f -> p u e f", u=2, e=2)
+    wd_view = wd.rearrange("(n p i) l -> p n i l", p=P, i=2)
+    cos_view = rope_cos.rearrange("(p j) r -> p j r", j=4)
+    sin_view = rope_sin.rearrange("(p j) r -> p j r", j=4)
+    out0_view = out_0.rearrange("b (p j) d -> b p j d", j=4)
+    out1_view = out_1.rearrange("(a p) l -> p a l", p=P)
+
+    with ExitStack() as ctx:
+        keep = ctx.enter_context(tc.tile_pool(name="keep", bufs=1))
+        raw = ctx.enter_context(tc.tile_pool(name="raw", bufs=7))
+        work = ctx.enter_context(tc.tile_pool(name="work", bufs=2))
+        psum = ctx.enter_context(tc.psum_pool(name="psum", bufs=8))
+
+        ident = keep.tile([P, P], F32, align_bytes=64)
+        make_identity(nc, ident[:])
+        warm = keep.tile([P, 16], F32, align_bytes=64)
+        nc.vector.memset(warm[:], 0.0)
+        warm2 = keep.tile([P, 16], F32, align_bytes=64)
+
+        cos_t = keep.tile([P, 4, DR], F32, align_bytes=64)
+        sin_t = keep.tile([P, 4, DR], F32, align_bytes=64)
+        wu_codes = keep.tile([P, PASSES, DL], U32, align_bytes=64)
+        wu_scales = keep.tile([P, PASSES, DL], U8, align_bytes=64)
+        wd_codes = keep.tile([P, D], U32, align_bytes=64)
+        wd_scales = keep.tile([P, D], U8, align_bytes=64)
+        x_codes = keep.tile([P, B, D], U32, align_bytes=64)
+        x_scales = keep.tile([P, B, D], U8, align_bytes=64)
+
+        with tc.manual_schedule():
+            nc.scalar.copy(out=warm2[:], in_=warm[:])
+
+            def load_g(k):
+                t = raw.tile([P, H, HF], BF16, name="g_raw", tag="rawa", align_bytes=64)
+                nc.sync.dma_start(out=t[:], in_=g[k // 4].rearrange("(p j) h f -> p j h f", j=4)[:, k % 4])
+                return t
+
+            def load_wu(u, half):
+                t = raw.tile([P, 2, J // 2], BF16, name="wu_raw", tag="rawa", align_bytes=64)
+                nc.sync.dma_start(out=t[:], in_=wu_view[:, u, :, half * (J // 2) : (half + 1) * (J // 2)])
+                return t
+
+            def load_wd(c):
+                t = raw.tile([P, 4, 2, DL], BF16, name="wd_raw", tag="rawb", bufs=4, align_bytes=64)
+                nc.sync.dma_start(out=t[:], in_=wd_view[:, 4 * c : 4 * c + 4])
+                return t
+
+            def load_x(half, b):
+                t = raw.tile([P, 4, D // 2], BF16, name="x_raw", tag="rawb", bufs=4, align_bytes=64)
+                nc.sync.dma_start(out=t[:], in_=x_view[b][:, :, half * (D // 2) : (half + 1) * (D // 2)])
+                return t
+
+            nc.sync.dma_start(out=cos_t[:], in_=cos_view)
+            nc.sync.dma_start(out=sin_t[:], in_=sin_view)
+            g0_parts = []
+            wu_raw = {}
+            g_raw = {}
+            wd_raw = {}
+            x_raw = {}
+            for half, wus in ((0, ((0, 0),)), (1, ((1, 0), (0, 1), (1, 1)))):
+                t = keep.tile([P, H // 2, HF], BF16, name=f"g0_{half}", align_bytes=64)
+                nc.sync.dma_start(out=t[:], in_=g[0].rearrange("(p j) h f -> p j h f", j=4)[:, 0, half * 8 : half * 8 + 8])
+                g0_parts.append(t)
+                for key in wus:
+                    wu_raw[key] = load_wu(*key)
+            for k in (1, 2, 3):
+                g_raw[k] = load_g(k)
+            wd_raw[0] = load_wd(0)
+            g_raw[4] = load_g(4)
+            wd_raw[1] = load_wd(1)
+            for k in (5, 6, 7):
+                g_raw[k] = load_g(k)
+            for half in range(2):
+                for b in range(B):
+                    x_raw[half, b] = load_x(half, b)
+
+            def new_bank():
+                return psum.tile([P, 512], F32, name="bank", tag="bank")
+
+            def rope_mul(parts, k):
+                res = []
+                for t in parts:
+                    heads = t.shape[1]
+                    gr = t[:, :, DH:HF]
+                    pc = work.tile([P, H, DR], F32, name="pc", tag="pc", bufs=2, align_bytes=64)
+                    ps = work.tile([P, H, DR], F32, name="ps", tag="ps", bufs=2, align_bytes=64)
+                    shape = [P, heads, DR]
+                    nc.vector.tensor_tensor(out=pc[:, :heads], in0=gr, in1=cos_t[:, k % 4, :].unsqueeze(1).to_broadcast(shape), op=MULT)
+                    nc.vector.tensor_tensor(out=ps[:, :heads], in0=gr, in1=sin_t[:, k % 4, :].unsqueeze(1).to_broadcast(shape), op=MULT)
+                    res.append((t, pc, ps, heads))
+                return res
+
+            def rope_add(items):
+                for t, pc, ps, n in items:
+                    nc.vector.tensor_tensor(out=t[:, :, DH : DH + 32], in0=pc[:, :n, 0:32], in1=ps[:, :n, 32:64], op=ADD)
+                    nc.vector.tensor_tensor(out=t[:, :, DH + 32 : HF], in0=pc[:, :n, 32:64], in1=ps[:, :n, 0:32], op=SUB)
+
+            def wu_bank(u, s):
+                src = wu_raw[u, s // 3]
+                bank = new_bank()
+                for e in range(2):
+                    words = src[:, e, (s % 3) * 512 : (s % 3 + 1) * 512].bitcast(F32)
+                    for w in range(2):
+                        q = 2 * e + w
+                        nc.tensor.transpose(bank[:, q * P : (q + 1) * P], words[:, w:256:2], ident[:])
+                grouped = work.tile([P, 1024], BF16, name="wu_grp", tag="wgrp", bufs=3, align_bytes=64)
+                nc.scalar.copy(
+                    out=grouped[:].bitcast(F32).rearrange("p (m e w) -> p m e w", e=2, w=2),
+                    in_=bank[:].rearrange("p (e w m) -> p m e w", e=2, w=2),
+                )
+                return u, s, grouped
+
+            def wu_quant(item):
+                u, s, grouped = item
+                nc.vector.quantize_mx(
+                    out=wu_codes[:, s, 256 * u : 256 * u + 256].bitcast(E4M3),
+                    scales=wu_scales[:, s, 256 * u : 256 * u + 256],
+                    in_=grouped[:],
+                )
+
+            def wd_bank(n):
+                src = wd_raw[n // 4]
+                bank = new_bank()
+                for i in range(2):
+                    words = src[:, n % 4, i, :].bitcast(F32)
+                    for w in range(2):
+                        q = 2 * i + w
+                        nc.tensor.transpose(bank[:, q * P : (q + 1) * P], words[:, w:256:2], ident[:])
+                grouped = work.tile([P, 1024], BF16, name="wd_grp", tag="wgrp", bufs=3, align_bytes=64)
+                nc.scalar.copy(
+                    out=grouped[:].bitcast(F32).rearrange("p (m i w) -> p m i w", i=2, w=2),
+                    in_=bank[:].rearrange("p (i w m) -> p m i w", i=2, w=2),
+                )
+                return n, grouped
+
+            def wd_quant(item):
+                n, grouped = item
+                nc.vector.quantize_mx(
+                    out=wd_codes[:, 256 * n : 256 * n + 256].bitcast(E4M3),
+                    scales=wd_scales[:, 256 * n : 256 * n + 256],
+                    in_=grouped[:],
+                )
+
+            def g_words(k, s):
+                if k == 0:
+                    flat = g0_parts[s // 3][:].rearrange("p h f -> p (h f)")
+                    s = s % 3
+                else:
+                    flat = g_raw[k][:].rearrange("p h f -> p (h f)")
+                return flat[:, 512 * s : 512 * s + 512].bitcast(F32)
+
+            def dz2_transpose(k):
+                grouped = work.tile([P, J], BF16, name="g_grp", tag="ggrp", bufs=2, align_bytes=64)
+                for c in range(3):
+                    bank = new_bank()
+                    for i in range(2):
+                        words = g_words(k, 2 * c + i)
+                        for w in range(2):
+                            q = 2 * i + w
+                            nc.tensor.transpose(bank[:, q * P : (q + 1) * P], words[:, w:256:2], ident[:])
+                    nc.scalar.copy(
+                        out=grouped[:, 1024 * c : 1024 * c + 1024].bitcast(F32).rearrange("p (i r w) -> p i r w", i=2, w=2),
+                        in_=bank[:].rearrange("p (i w r) -> p i r w", i=2, w=2),
+                    )
+                return grouped
+
+            dz2 = {}
+
+            def dz2_quant(k, grouped):
+                codes = work.tile([P, PASSES, P], U32, name="dz2_codes", tag="dz2c", bufs=3, align_bytes=64)
+                scales = work.tile([P, PASSES, P], U8, name="dz2_scales", tag="dz2s", bufs=3, align_bytes=64)
+                for a, b in ((0, 4), (4, 6)):
+                    nc.vector.quantize_mx(
+                        out=codes[:, a:b, :].rearrange("p s r -> p (s r)").bitcast(E5M2),
+                        scales=scales[:, a:b, :].rearrange("p s r -> p (s r)"),
+                        in_=grouped[:, 512 * a : 512 * b],
+                    )
+                dz2[k] = (codes, scales)
+
+            dz1_tok = {}
+            acc = {}
+
+            def stage1(k, lo=0, hi=PASSES):
+                codes, scales = dz2[k]
+                if lo == 0:
+                    acc[k] = new_bank()
+                for s in range(lo, hi):
+                    nc.tensor.matmul_mx(
+                        out=acc[k][:],
+                        lhsT=codes[:, s, :].bitcast(E5M2),
+                        lhsT_scale=scales[:, s, :],
+                        rhs=wu_codes[:, s, :].bitcast(E4M3),
+                        rhs_scale=wu_scales[:, s, :],
+                        start=(s == 0),
+                        stop=(s == PASSES - 1),
+                    )
+
+            def stage1_copy(k):
+                if k % GTILES == 0:
+                    dz1_tok[k // GTILES] = work.tile([P, GTILES, DL], BF16, name="dz1_tok", tag="dz1t", bufs=2, align_bytes=64)
+                nc.scalar.copy(out=dz1_tok[k // GTILES][:, k % GTILES, :], in_=acc[k][:])
+
+            dz1f_grp = {}
+
+            def dz1_transpose(k):
+                words = dz1_tok[k // GTILES][:, k % GTILES, :].bitcast(F32)
+                bank = new_bank()
+                for u in range(2):
+                    nc.tensor.transpose(bank[:, u * P : (u + 1) * P], words[:, u * P : (u + 1) * P], ident[:])
+                grouped = work.tile([P, DL], BF16, name="dz1f_grp", tag="dz1fg", bufs=2, align_bytes=64)
+                nc.scalar.copy(
+                    out=grouped[:].bitcast(F32).rearrange("p (r u) -> p r u", u=2),
+                    in_=bank[:, : 2 * P].rearrange("p (u r) -> p r u", u=2),
+                )
+                dz1f_grp[k] = grouped
+
+            dz1f = {}
+
+            def dz1f_quant(k):
+                codes = work.tile([P, P], U32, name="dz1f_codes", tag="dz1fc", bufs=3, align_bytes=64)
+                scales = work.tile([P, P], U8, name="dz1f_scales", tag="dz1fs", bufs=3, align_bytes=64)
+                nc.vector.quantize_mx(out=codes[:].bitcast(E5M2), scales=scales[:], in_=dz1f_grp[k][:])
+                dz1f[k] = (codes, scales)
+
+            def out0_tile(k):
+                codes, scales = dz1f[k]
+                res = work.tile([P, D], F32, name="res0", tag="res0", bufs=2, align_bytes=64)
+                for n in range(4):
+                    bank = new_bank()
+                    nc.tensor.matmul_mx(
+                        out=bank[:],
+                        lhsT=codes[:].bitcast(E5M2),
+                        lhsT_scale=scales[:],
+                        rhs=wd_codes[:, 512 * n : 512 * n + 512].bitcast(E4M3),
+                        rhs_scale=wd_scales[:, 512 * n : 512 * n + 512],
+                        start=True,
+                        stop=True,
+                    )
+                    nc.scalar.copy(out=res[:, 512 * n : 512 * n + 512], in_=bank[:])
+                nc.sync.dma_start(out=out0_view[k // GTILES][:, k % GTILES, :], in_=res[:])
+
+            dz1 = {}
+            dz1_grp = {}
+
+            def interleave(engine, dst, src):
+                out = dst.rearrange("p (c i) t -> p c t i", i=4)
+                in_ = src.rearrange("p t (c i) -> p c t i", i=4)
+                if engine == "v":
+                    nc.vector.tensor_copy(out=out, in_=in_)
+                else:
+                    nc.scalar.copy(out=out, in_=in_)
+
+            def dz1_interleave(b):
+                grouped = work.tile([P, DL, 4], BF16, name="dz1_grp", tag="xgrp", bufs=3, align_bytes=64)
+                interleave("v", grouped[:], dz1_tok[b][:])
+                dz1_grp[b] = grouped
+
+            def dz1_quant(b):
+                codes = keep.tile([P, DL], U32, name=f"dz1_codes{b}", align_bytes=64)
+                scales = keep.tile([P, DL], U8, name=f"dz1_scales{b}", align_bytes=64)
+                nc.vector.quantize_mx(
+                    out=codes[:].bitcast(E5M2), scales=scales[:], in_=dz1_grp[b][:].rearrange("p c t -> p (c t)")
+                )
+                dz1[b] = (codes, scales)
+
+            x_grp = {}
+
+            def x_interleave(engine, n, b):
+                grouped = work.tile([P, 512, 4], BF16, name="x_grp", tag="xgrp", bufs=3, align_bytes=64)
+                interleave(engine, grouped[:], x_raw[n // 2, b][:, :, 512 * (n % 2) : 512 * (n % 2) + 512])
+                x_grp[n, b] = grouped
+
+            def x_quant(n, b):
+                nc.vector.quantize_mx(
+                    out=x_codes[:, b, 512 * n : 512 * n + 512].bitcast(E4M3),
+                    scales=x_scales[:, b, 512 * n : 512 * n + 512],
+                    in_=x_grp[n, b][:].rearrange("p c t -> p (c t)"),
+                )
+
+            def out1_tile(a, engine):
+                bank = new_bank()
+                for b in range(B):
+                    codes, scales = dz1[b]
+                    nc.tensor.matmul_mx(
+                        out=bank[:],
+                        lhsT=x_codes[:, b, P * a : P * a + P].bitcast(E4M3),
+                        lhsT_scale=x_scales[:, b, P * a : P * a + P],
+                        rhs=codes[:].bitcast(E5M2),
+                        rhs_scale=scales[:],
+                        start=(b == 0),
+                        stop=(b == B - 1),
+                    )
+                res = work.tile([P, DL], F32, name="res1", tag="res1", bufs=6, align_bytes=64)
+                out = res[:].rearrange("p (m u e) -> p m u e", u=2, e=2)
+                in_ = bank[:].rearrange("p (u m e) -> p m u e", u=2, e=2)
+                if engine == "v":
+                    nc.vector.tensor_copy(out=out, in_=in_)
+                else:
+                    nc.scalar.copy(out=out, in_=in_)
+                nc.sync.dma_start(out=out1_view[:, a, :], in_=res[:])
+
+            grp = {}
+            ropes = {}
+
+            i0 = rope_mul(g0_parts[:1], 0)
+            w00 = [wu_bank(0, s) for s in range(3)]
+            rope_add(i0)
+            i1 = rope_mul(g0_parts[1:], 0)
+            wu_quant(w00[0])
+            rope_add(i1)
+            wu_quant(w00[1])
+            wu_quant(w00[2])
+            w10 = [wu_bank(1, s) for s in range(3)]
+            grp[0] = dz2_transpose(0)
+            for item in w10:
+                wu_quant(item)
+            w01 = [wu_bank(0, s) for s in range(3, 6)]
+            dz2_quant(0, grp[0])
+            stage1(0, 0, 3)
+            w11 = [wu_bank(1, s) for s in range(3, 6)]
+            for item in w01:
+                wu_quant(item)
+            ropes[1] = rope_mul([g_raw[1]], 1)
+            for item in w11:
+                wu_quant(item)
+            rope_add(ropes[1])
+            ropes[2] = rope_mul([g_raw[2]], 2)
+            stage1(0, 3, 6)
+            stage1_copy(0)
+            x_order = [(n, b) for n in range(4) for b in range(B)]
+            x_done = []
+            for k in range(TILES + 2):
+                if k + 1 < TILES:
+                    grp[k + 1] = dz2_transpose(k + 1)
+                wds = []
+                if k < 2:
+                    for n in range(4 * k, 4 * k + 2):
+                        wds.append(wd_bank(n))
+                if 1 <= k <= TILES:
+                    dz1_transpose(k - 1)
+                if 1 <= k < TILES:
+                    stage1(k)
+                    stage1_copy(k)
+                if k + 2 in ropes:
+                    rope_add(ropes[k + 2])
+                if k + 3 < TILES:
+                    ropes[k + 3] = rope_mul([g_raw[k + 3]], k + 3)
+                for item in wds:
+                    wd_quant(item)
+                if k < 2:
+                    for n in range(4 * k + 2, 4 * k + 4):
+                        wds.append(wd_bank(n))
+                if k + 1 < TILES:
+                    dz2_quant(k + 1, grp[k + 1])
+                if k < 2:
+                    for item in wds[2:]:
+                        wd_quant(item)
+                if 1 <= k <= TILES:
+                    dz1f_quant(k - 1)
+                if 2 <= k:
+                    out0_tile(k - 2)
+                if k == 4:
+                    dz1_interleave(0)
+                    x_interleave("v", 0, 0)
+                    dz1_quant(0)
+                if k == 5:
+                    x_interleave("v", 0, 1)
+                    x_quant(0, 0)
+                    x_interleave("v", 1, 0)
+                    x_quant(0, 1)
+                if k == 6:
+                    x_interleave("v", 1, 1)
+                    x_quant(1, 0)
+                    x_interleave("v", 2, 0)
+                    x_quant(1, 1)
+                if k == 7:
+                    x_interleave("s", 3, 0)
+                    x_interleave("v", 2, 1)
+                    x_quant(2, 0)
+                    dz1_interleave(1)
+                    x_quant(2, 1)
+                    dz1_quant(1)
+                    x_quant(3, 0)
+                if k == 8:
+                    x_interleave("v", 3, 1)
+                    for a in range(4):
+                        out1_tile(a, "v" if a % 2 else "s")
+                    x_quant(3, 1)
+            for a in range(4, 16):
+                out1_tile(a, "v" if a % 2 else "s")

@@ -41,7 +41,9 @@ def tile_multilatentattention_pb_v_kernel(tc, x, wd, wu, rope_cos, rope_sin, g, 
         keep = ctx.enter_context(tc.tile_pool(name="keep", bufs=1))
         raw = ctx.enter_context(tc.tile_pool(name="raw", bufs=7))
         work = ctx.enter_context(tc.tile_pool(name="work", bufs=2))
-        psum = ctx.enter_context(tc.psum_pool(name="psum", bufs=8))
+        psum = ctx.enter_context(tc.psum_pool(name="psum", bufs=7))
+        tables = ctx.enter_context(tc.psum_pool(name="tables", bufs=1))
+        tab_bank = tables.tile([P, 512], F32)
 
         ident = keep.tile([P, P], F32, align_bytes=64)
         make_identity(nc, ident[:])
@@ -81,32 +83,65 @@ def tile_multilatentattention_pb_v_kernel(tc, x, wd, wu, rope_cos, rope_sin, g, 
                 nc.sync.dma_start(out=t[:], in_=x_view[b][:, :, half * (D // 2) : (half + 1) * (D // 2)])
                 return t
 
-            nc.sync.dma_start(out=cos_t[:], in_=cos_view)
-            nc.sync.dma_start(out=sin_t[:], in_=sin_view)
-            g0_parts = []
             wu_raw = {}
             g_raw = {}
             wd_raw = {}
             x_raw = {}
-            for half, wus in ((0, ((0, 0),)), (1, ((1, 0), (0, 1), (1, 1)))):
+            g0_parts = []
+
+            def load_g0(half):
                 t = keep.tile([P, H // 2, HF], BF16, name=f"g0_{half}", align_bytes=64)
                 nc.sync.dma_start(out=t[:], in_=g[0].rearrange("(p j) h f -> p j h f", j=4)[:, 0, half * 8 : half * 8 + 8])
                 g0_parts.append(t)
-                for key in wus:
-                    wu_raw[key] = load_wu(*key)
-            for k in (1, 2, 3):
-                g_raw[k] = load_g(k)
-            wd_raw[0] = load_wd(0)
-            g_raw[4] = load_g(4)
-            wd_raw[1] = load_wd(1)
-            for k in (5, 6, 7):
+
+            wu_raw[0, 0] = load_wu(0, 0)
+            nc.sync.dma_start(out=cos_t[:], in_=cos_view)
+            nc.sync.dma_start(out=sin_t[:], in_=sin_view)
+            load_g0(0)
+            load_g0(1)
+            wu_raw[1, 0] = load_wu(1, 0)
+            g_raw[1] = load_g(1)
+            wu_raw[0, 1] = load_wu(0, 1)
+            wu_raw[1, 1] = load_wu(1, 1)
+            for c in range(2):
+                wd_raw[c] = load_wd(c)
+                g_raw[2 + c] = load_g(2 + c)
+            for k in range(4, TILES):
                 g_raw[k] = load_g(k)
             for half in range(2):
                 for b in range(B):
                     x_raw[half, b] = load_x(half, b)
 
+            def copy_out(engine, out, in_):
+                if engine == "v":
+                    nc.vector.tensor_copy(out=out, in_=in_)
+                else:
+                    nc.scalar.copy(out=out, in_=in_)
+
             def new_bank():
                 return psum.tile([P, 512], F32, name="bank", tag="bank")
+
+            grp = {}
+            ropes = {}
+
+            def cos_of(k):
+                return cos_t[:, k, :] if k == 0 else tab_bank[:, DR * (k % 4) : DR * (k % 4) + DR]
+
+            def sin_of(k):
+                return sin_t[:, k, :] if k == 0 else tab_bank[:, 256 + DR * (k % 4) : 256 + DR * (k % 4) + DR]
+
+            turned_sb = keep.tile([P, 512], F32, align_bytes=64)
+
+            def turn_tables():
+                turned = new_bank()
+                for i in range(4):
+                    flat = (cos_t, sin_t)[i // 2][:].rearrange("p j r -> p (j r)")
+                    nc.tensor.transpose(turned[:, i * P : (i + 1) * P], flat[:, (i % 2) * P : (i % 2 + 1) * P], ident[:])
+                nc.scalar.copy(out=turned_sb[:], in_=turned[:])
+
+            def turn_tables_back():
+                for i in range(4):
+                    nc.tensor.transpose(tab_bank[:, i * P : (i + 1) * P], turned_sb[:, i * P : (i + 1) * P], ident[:])
 
             def rope_mul(parts, k):
                 res = []
@@ -116,15 +151,16 @@ def tile_multilatentattention_pb_v_kernel(tc, x, wd, wu, rope_cos, rope_sin, g, 
                     pc = work.tile([P, H, DR], F32, name="pc", tag="pc", bufs=2, align_bytes=64)
                     ps = work.tile([P, H, DR], F32, name="ps", tag="ps", bufs=2, align_bytes=64)
                     shape = [P, heads, DR]
-                    nc.vector.tensor_tensor(out=pc[:, :heads], in0=gr, in1=cos_t[:, k % 4, :].unsqueeze(1).to_broadcast(shape), op=MULT)
-                    nc.vector.tensor_tensor(out=ps[:, :heads], in0=gr, in1=sin_t[:, k % 4, :].unsqueeze(1).to_broadcast(shape), op=MULT)
+                    nc.vector.tensor_tensor(out=pc[:, :heads], in0=gr, in1=cos_of(k).unsqueeze(1).to_broadcast(shape), op=MULT)
+                    nc.vector.tensor_tensor(out=ps[:, :heads], in0=gr, in1=sin_of(k).unsqueeze(1).to_broadcast(shape), op=MULT)
                     res.append((t, pc, ps, heads))
                 return res
 
-            def rope_add(items):
+            def rope_add(items, k):
+                eng = nc.gpsimd if k in (4, 6) else nc.vector
                 for t, pc, ps, n in items:
-                    nc.vector.tensor_tensor(out=t[:, :, DH : DH + 32], in0=pc[:, :n, 0:32], in1=ps[:, :n, 32:64], op=ADD)
-                    nc.vector.tensor_tensor(out=t[:, :, DH + 32 : HF], in0=pc[:, :n, 32:64], in1=ps[:, :n, 0:32], op=SUB)
+                    eng.tensor_tensor(out=t[:, :, DH : DH + 32], in0=pc[:, :n, 0:32], in1=ps[:, :n, 32:64], op=ADD)
+                    eng.tensor_tensor(out=t[:, :, DH + 32 : HF], in0=pc[:, :n, 32:64], in1=ps[:, :n, 0:32], op=SUB)
 
             def wu_bank(u, s):
                 src = wu_raw[u, s // 3]
@@ -180,20 +216,22 @@ def tile_multilatentattention_pb_v_kernel(tc, x, wd, wu, rope_cos, rope_sin, g, 
                     flat = g_raw[k][:].rearrange("p h f -> p (h f)")
                 return flat[:, 512 * s : 512 * s + 512].bitcast(F32)
 
-            def dz2_transpose(k):
-                grouped = work.tile([P, J], BF16, name="g_grp", tag="ggrp", bufs=2, align_bytes=64)
-                for c in range(3):
-                    bank = new_bank()
-                    for i in range(2):
-                        words = g_words(k, 2 * c + i)
-                        for w in range(2):
-                            q = 2 * i + w
-                            nc.tensor.transpose(bank[:, q * P : (q + 1) * P], words[:, w:256:2], ident[:])
-                    nc.scalar.copy(
-                        out=grouped[:, 1024 * c : 1024 * c + 1024].bitcast(F32).rearrange("p (i r w) -> p i r w", i=2, w=2),
-                        in_=bank[:].rearrange("p (i w r) -> p i r w", i=2, w=2),
-                    )
-                return grouped
+            def dz2_bank(k, c):
+                if c == 0:
+                    grp[k] = work.tile([P, J], BF16, name="g_grp", tag="ggrp", bufs=2, align_bytes=64)
+                bank = new_bank()
+                for i in range(2):
+                    words = g_words(k, 2 * c + i)
+                    for w in range(2):
+                        q = 2 * i + w
+                        nc.tensor.transpose(bank[:, q * P : (q + 1) * P], words[:, w:256:2], ident[:])
+                return bank
+
+            def dz2_copy(k, c, bank):
+                nc.scalar.copy(
+                    out=grp[k][:, 1024 * c : 1024 * c + 1024].bitcast(F32).rearrange("p (i r w) -> p i r w", i=2, w=2),
+                    in_=bank[:].rearrange("p (i w r) -> p i r w", i=2, w=2),
+                )
 
             dz2 = {}
 
@@ -253,22 +291,26 @@ def tile_multilatentattention_pb_v_kernel(tc, x, wd, wu, rope_cos, rope_sin, g, 
                 nc.vector.quantize_mx(out=codes[:].bitcast(E5M2), scales=scales[:], in_=dz1f_grp[k][:])
                 dz1f[k] = (codes, scales)
 
-            def out0_tile(k):
+            res0 = {}
+
+            def out0_part(k, n, engine):
                 codes, scales = dz1f[k]
-                res = work.tile([P, D], F32, name="res0", tag="res0", bufs=2, align_bytes=64)
-                for n in range(4):
-                    bank = new_bank()
-                    nc.tensor.matmul_mx(
-                        out=bank[:],
-                        lhsT=codes[:].bitcast(E5M2),
-                        lhsT_scale=scales[:],
-                        rhs=wd_codes[:, 512 * n : 512 * n + 512].bitcast(E4M3),
-                        rhs_scale=wd_scales[:, 512 * n : 512 * n + 512],
-                        start=True,
-                        stop=True,
-                    )
-                    nc.scalar.copy(out=res[:, 512 * n : 512 * n + 512], in_=bank[:])
-                nc.sync.dma_start(out=out0_view[k // GTILES][:, k % GTILES, :], in_=res[:])
+                if n == 0:
+                    res0[k] = work.tile([P, D], F32, name="res0", tag="res0", bufs=2, align_bytes=64)
+                bank = new_bank()
+                nc.tensor.matmul_mx(
+                    out=bank[:],
+                    lhsT=codes[:].bitcast(E5M2),
+                    lhsT_scale=scales[:],
+                    rhs=wd_codes[:, 512 * n : 512 * n + 512].bitcast(E4M3),
+                    rhs_scale=wd_scales[:, 512 * n : 512 * n + 512],
+                    start=True,
+                    stop=True,
+                )
+                copy_out(engine, res0[k][:, 512 * n : 512 * n + 512], bank[:])
+                if n % 2 == 1:
+                    lo = 1024 * (n // 2)
+                    nc.sync.dma_start(out=out0_view[k // GTILES][:, k % GTILES, lo : lo + 1024], in_=res0[k][:, lo : lo + 1024])
 
             dz1 = {}
             dz1_grp = {}
@@ -308,7 +350,11 @@ def tile_multilatentattention_pb_v_kernel(tc, x, wd, wu, rope_cos, rope_sin, g, 
                     in_=x_grp[n, b][:].rearrange("p c t -> p (c t)"),
                 )
 
+            res1 = {}
+
             def out1_tile(a, engine):
+                if a % 2 == 0:
+                    res1[a // 2] = work.tile([P, 2, DL], F32, name="res1", tag="res1", bufs=4, align_bytes=64)
                 bank = new_bank()
                 for b in range(B):
                     codes, scales = dz1[b]
@@ -321,101 +367,103 @@ def tile_multilatentattention_pb_v_kernel(tc, x, wd, wu, rope_cos, rope_sin, g, 
                         start=(b == 0),
                         stop=(b == B - 1),
                     )
-                res = work.tile([P, DL], F32, name="res1", tag="res1", bufs=6, align_bytes=64)
-                out = res[:].rearrange("p (m u e) -> p m u e", u=2, e=2)
+                res = res1[a // 2][:, a % 2, :]
+                out = res.rearrange("p (m u e) -> p m u e", u=2, e=2)
                 in_ = bank[:].rearrange("p (u m e) -> p m u e", u=2, e=2)
                 if engine == "v":
                     nc.vector.tensor_copy(out=out, in_=in_)
                 else:
                     nc.scalar.copy(out=out, in_=in_)
-                nc.sync.dma_start(out=out1_view[:, a, :], in_=res[:])
+                if a % 2 == 1:
+                    nc.sync.dma_start(out=out1_view[:, a - 1 : a + 1, :], in_=res1[a // 2][:])
 
-            grp = {}
-            ropes = {}
+            def rope(k):
+                rope_add(rope_mul([g_raw[k]], k), k)
 
-            i0 = rope_mul(g0_parts[:1], 0)
+            def dz2_step(k, cs):
+                for c in cs:
+                    dz2_copy(k, c, dz2_bank(k, c))
+
+            xs = [(n, b) for n in range(4) for b in range(B)]
+            pend = []
+
+            def x_step():
+                xu = xs.pop(0)
+                x_interleave("v", *xu)
+                if pend:
+                    x_quant(*pend.pop())
+                pend.append(xu)
+
             w00 = [wu_bank(0, s) for s in range(3)]
-            rope_add(i0)
-            i1 = rope_mul(g0_parts[1:], 0)
-            wu_quant(w00[0])
-            rope_add(i1)
-            wu_quant(w00[1])
-            wu_quant(w00[2])
+            turn_tables()
+            turn_tables_back()
+            rope_add(rope_mul(g0_parts[:1], 0), 0)
             w10 = [wu_bank(1, s) for s in range(3)]
-            grp[0] = dz2_transpose(0)
+            dz2_step(0, (0,))
+            for item in w00:
+                wu_quant(item)
+            rope_add(rope_mul(g0_parts[1:], 0), 0)
             for item in w10:
                 wu_quant(item)
+            dz2_step(0, (1, 2))
+            rope(1)
             w01 = [wu_bank(0, s) for s in range(3, 6)]
             dz2_quant(0, grp[0])
-            stage1(0, 0, 3)
-            w11 = [wu_bank(1, s) for s in range(3, 6)]
             for item in w01:
                 wu_quant(item)
-            ropes[1] = rope_mul([g_raw[1]], 1)
+            w11 = [wu_bank(1, s) for s in range(3, 6)]
             for item in w11:
                 wu_quant(item)
-            rope_add(ropes[1])
-            ropes[2] = rope_mul([g_raw[2]], 2)
-            stage1(0, 3, 6)
-            stage1_copy(0)
-            x_order = [(n, b) for n in range(4) for b in range(B)]
-            x_done = []
-            for k in range(TILES + 2):
+            ropes_at = {0: (2,), 1: (3,), 2: (4, 5), 3: (6, 7)}
+            for k in range(TILES):
                 if k + 1 < TILES:
-                    grp[k + 1] = dz2_transpose(k + 1)
-                wds = []
-                if k < 2:
-                    for n in range(4 * k, 4 * k + 2):
-                        wds.append(wd_bank(n))
-                if 1 <= k <= TILES:
+                    dz2_step(k + 1, (0, 1))
+                    bank = dz2_bank(k + 1, 2)
+                if k >= 1:
                     dz1_transpose(k - 1)
-                if 1 <= k < TILES:
+                if k + 1 < TILES:
+                    dz2_copy(k + 1, 2, bank)
+                for j in ropes_at.get(k, ())[:1]:
+                    rope(j)
+                if k >= 1:
+                    dz1f_quant(k - 1)
+                for j in ropes_at.get(k, ())[1:]:
+                    rope(j)
+                if k >= 1:
                     stage1(k)
                     stage1_copy(k)
-                if k + 2 in ropes:
-                    rope_add(ropes[k + 2])
-                if k + 3 < TILES:
-                    ropes[k + 3] = rope_mul([g_raw[k + 3]], k + 3)
-                for item in wds:
-                    wd_quant(item)
+                wds = []
                 if k < 2:
-                    for n in range(4 * k + 2, 4 * k + 4):
+                    for n in range(4 * k, 4 * k + 4):
                         wds.append(wd_bank(n))
+                        if len(wds) == 3:
+                            wd_quant(wds.pop(0))
+                if k == 0:
+                    stage1(k)
+                    stage1_copy(k)
                 if k + 1 < TILES:
                     dz2_quant(k + 1, grp[k + 1])
-                if k < 2:
-                    for item in wds[2:]:
-                        wd_quant(item)
-                if 1 <= k <= TILES:
-                    dz1f_quant(k - 1)
-                if 2 <= k:
-                    out0_tile(k - 2)
+                for item in wds:
+                    wd_quant(item)
                 if k == 4:
                     dz1_interleave(0)
-                    x_interleave("v", 0, 0)
+                if 3 <= k <= 6:
+                    x_step()
+                if k == 4:
                     dz1_quant(0)
-                if k == 5:
-                    x_interleave("v", 0, 1)
-                    x_quant(0, 0)
-                    x_interleave("v", 1, 0)
-                    x_quant(0, 1)
-                if k == 6:
-                    x_interleave("v", 1, 1)
-                    x_quant(1, 0)
-                    x_interleave("v", 2, 0)
-                    x_quant(1, 1)
-                if k == 7:
-                    x_interleave("s", 3, 0)
-                    x_interleave("v", 2, 1)
-                    x_quant(2, 0)
-                    dz1_interleave(1)
-                    x_quant(2, 1)
-                    dz1_quant(1)
-                    x_quant(3, 0)
-                if k == 8:
-                    x_interleave("v", 3, 1)
-                    for a in range(4):
-                        out1_tile(a, "v" if a % 2 else "s")
-                    x_quant(3, 1)
-            for a in range(4, 16):
-                out1_tile(a, "v" if a % 2 else "s")
+                for j in (0, 1) if k == 2 else (k - 1,) if k > 2 else ():
+                    for n in range(4):
+                        out0_part(j, n, "v" if n == 3 and k in (5, 6) else "s")
+                        if k == 7 and n == 1:
+                            dz1_transpose(7)
+            dz1_interleave(1)
+            dz1f_quant(7)
+            dz1_quant(1)
+            for n in range(4):
+                out0_part(7, n, "s")
+            for a in range(16):
+                while len(xs) > 0 and xs[0][0] <= (a + 4) // 4:
+                    x_step()
+                if len(pend) > 0 and (pend[0][0] <= a // 4 or len(xs) == 0):
+                    x_quant(*pend.pop())
+                out1_tile(a, "v" if a in (12, 14) else "s")

@@ -41,9 +41,7 @@ def tile_multilatentattention_pb_v_kernel(tc, x, wd, wu, rope_cos, rope_sin, g, 
         keep = ctx.enter_context(tc.tile_pool(name="keep", bufs=1))
         raw = ctx.enter_context(tc.tile_pool(name="raw", bufs=7))
         work = ctx.enter_context(tc.tile_pool(name="work", bufs=2))
-        psum = ctx.enter_context(tc.psum_pool(name="psum", bufs=7))
-        tables = ctx.enter_context(tc.psum_pool(name="tables", bufs=1))
-        tab_bank = tables.tile([P, 512], F32)
+        psum = ctx.enter_context(tc.psum_pool(name="psum", bufs=8))
 
         ident = keep.tile([P, P], F32, align_bytes=64)
         make_identity(nc, ident[:])
@@ -94,9 +92,9 @@ def tile_multilatentattention_pb_v_kernel(tc, x, wd, wu, rope_cos, rope_sin, g, 
                 nc.sync.dma_start(out=t[:], in_=g[0].rearrange("(p j) h f -> p j h f", j=4)[:, 0, half * 8 : half * 8 + 8])
                 g0_parts.append(t)
 
-            wu_raw[0, 0] = load_wu(0, 0)
             nc.sync.dma_start(out=cos_t[:], in_=cos_view)
             nc.sync.dma_start(out=sin_t[:], in_=sin_view)
+            wu_raw[0, 0] = load_wu(0, 0)
             load_g0(0)
             load_g0(1)
             wu_raw[1, 0] = load_wu(1, 0)
@@ -104,8 +102,8 @@ def tile_multilatentattention_pb_v_kernel(tc, x, wd, wu, rope_cos, rope_sin, g, 
             wu_raw[0, 1] = load_wu(0, 1)
             wu_raw[1, 1] = load_wu(1, 1)
             for c in range(2):
-                wd_raw[c] = load_wd(c)
                 g_raw[2 + c] = load_g(2 + c)
+                wd_raw[c] = load_wd(c)
             for k in range(4, TILES):
                 g_raw[k] = load_g(k)
             for half in range(2):
@@ -124,25 +122,6 @@ def tile_multilatentattention_pb_v_kernel(tc, x, wd, wu, rope_cos, rope_sin, g, 
             grp = {}
             ropes = {}
 
-            def cos_of(k):
-                return cos_t[:, k, :] if k == 0 else tab_bank[:, DR * (k % 4) : DR * (k % 4) + DR]
-
-            def sin_of(k):
-                return sin_t[:, k, :] if k == 0 else tab_bank[:, 256 + DR * (k % 4) : 256 + DR * (k % 4) + DR]
-
-            turned_sb = keep.tile([P, 512], F32, align_bytes=64)
-
-            def turn_tables():
-                turned = new_bank()
-                for i in range(4):
-                    flat = (cos_t, sin_t)[i // 2][:].rearrange("p j r -> p (j r)")
-                    nc.tensor.transpose(turned[:, i * P : (i + 1) * P], flat[:, (i % 2) * P : (i % 2 + 1) * P], ident[:])
-                nc.scalar.copy(out=turned_sb[:], in_=turned[:])
-
-            def turn_tables_back():
-                for i in range(4):
-                    nc.tensor.transpose(tab_bank[:, i * P : (i + 1) * P], turned_sb[:, i * P : (i + 1) * P], ident[:])
-
             def rope_mul(parts, k):
                 res = []
                 for t in parts:
@@ -151,16 +130,15 @@ def tile_multilatentattention_pb_v_kernel(tc, x, wd, wu, rope_cos, rope_sin, g, 
                     pc = work.tile([P, H, DR], F32, name="pc", tag="pc", bufs=2, align_bytes=64)
                     ps = work.tile([P, H, DR], F32, name="ps", tag="ps", bufs=2, align_bytes=64)
                     shape = [P, heads, DR]
-                    nc.vector.tensor_tensor(out=pc[:, :heads], in0=gr, in1=cos_of(k).unsqueeze(1).to_broadcast(shape), op=MULT)
-                    nc.vector.tensor_tensor(out=ps[:, :heads], in0=gr, in1=sin_of(k).unsqueeze(1).to_broadcast(shape), op=MULT)
+                    nc.vector.tensor_tensor(out=pc[:, :heads], in0=gr, in1=cos_t[:, k % 4, :].unsqueeze(1).to_broadcast(shape), op=MULT)
+                    nc.vector.tensor_tensor(out=ps[:, :heads], in0=gr, in1=sin_t[:, k % 4, :].unsqueeze(1).to_broadcast(shape), op=MULT)
                     res.append((t, pc, ps, heads))
                 return res
 
             def rope_add(items, k):
-                eng = nc.gpsimd if k in (4, 6) else nc.vector
                 for t, pc, ps, n in items:
-                    eng.tensor_tensor(out=t[:, :, DH : DH + 32], in0=pc[:, :n, 0:32], in1=ps[:, :n, 32:64], op=ADD)
-                    eng.tensor_tensor(out=t[:, :, DH + 32 : HF], in0=pc[:, :n, 32:64], in1=ps[:, :n, 0:32], op=SUB)
+                    nc.vector.tensor_tensor(out=t[:, :, DH : DH + 32], in0=pc[:, :n, 0:32], in1=ps[:, :n, 32:64], op=ADD)
+                    nc.vector.tensor_tensor(out=t[:, :, DH + 32 : HF], in0=pc[:, :n, 32:64], in1=ps[:, :n, 0:32], op=SUB)
 
             def wu_bank(u, s):
                 src = wu_raw[u, s // 3]
@@ -395,13 +373,12 @@ def tile_multilatentattention_pb_v_kernel(tc, x, wd, wu, rope_cos, rope_sin, g, 
                 pend.append(xu)
 
             w00 = [wu_bank(0, s) for s in range(3)]
-            turn_tables()
-            turn_tables_back()
             rope_add(rope_mul(g0_parts[:1], 0), 0)
-            w10 = [wu_bank(1, s) for s in range(3)]
+            w10 = []
+            for s in range(3):
+                wu_quant(w00[s])
+                w10.append(wu_bank(1, s))
             dz2_step(0, (0,))
-            for item in w00:
-                wu_quant(item)
             rope_add(rope_mul(g0_parts[1:], 0), 0)
             for item in w10:
                 wu_quant(item)
@@ -409,15 +386,21 @@ def tile_multilatentattention_pb_v_kernel(tc, x, wd, wu, rope_cos, rope_sin, g, 
             rope(1)
             w01 = [wu_bank(0, s) for s in range(3, 6)]
             dz2_quant(0, grp[0])
-            for item in w01:
-                wu_quant(item)
-            w11 = [wu_bank(1, s) for s in range(3, 6)]
+            w11 = []
+            for s in range(3):
+                wu_quant(w01[s])
+                w11.append(wu_bank(1, 3 + s))
             for item in w11:
                 wu_quant(item)
-            ropes_at = {0: (2,), 1: (3,), 2: (4, 5), 3: (6, 7)}
+            ropes_at = {0: (2,), 1: (3, 4), 2: (5,), 3: (6,), 4: (7,)}
+            left = None
             for k in range(TILES):
                 if k + 1 < TILES:
                     dz2_step(k + 1, (0, 1))
+                if k >= 2:
+                    for n in range(4):
+                        out0_part(k - 2, n, "v" if n == 3 and k in (5, 7) else "s")
+                if k + 1 < TILES:
                     bank = dz2_bank(k + 1, 2)
                 if k >= 1:
                     dz1_transpose(k - 1)
@@ -425,6 +408,9 @@ def tile_multilatentattention_pb_v_kernel(tc, x, wd, wu, rope_cos, rope_sin, g, 
                     dz2_copy(k + 1, 2, bank)
                 for j in ropes_at.get(k, ())[:1]:
                     rope(j)
+                if k == 6:
+                    x_step()
+                    x_step()
                 if k >= 1:
                     dz1f_quant(k - 1)
                 for j in ropes_at.get(k, ())[1:]:
@@ -447,15 +433,14 @@ def tile_multilatentattention_pb_v_kernel(tc, x, wd, wu, rope_cos, rope_sin, g, 
                     wd_quant(item)
                 if k == 4:
                     dz1_interleave(0)
-                if 3 <= k <= 6:
+                if k in (4, 6):
                     x_step()
                 if k == 4:
                     dz1_quant(0)
-                for j in (0, 1) if k == 2 else (k - 1,) if k > 2 else ():
-                    for n in range(4):
-                        out0_part(j, n, "v" if n == 3 and k in (5, 6) else "s")
-                        if k == 7 and n == 1:
-                            dz1_transpose(7)
+            for n in range(4):
+                out0_part(6, n, "s")
+                if n == 1:
+                    dz1_transpose(7)
             dz1_interleave(1)
             dz1f_quant(7)
             dz1_quant(1)
@@ -466,4 +451,4 @@ def tile_multilatentattention_pb_v_kernel(tc, x, wd, wu, rope_cos, rope_sin, g, 
                     x_step()
                 if len(pend) > 0 and (pend[0][0] <= a // 4 or len(xs) == 0):
                     x_quant(*pend.pop())
-                out1_tile(a, "v" if a in (12, 14) else "s")
+                out1_tile(a, "v" if a in (11, 12, 14) else "s")

@@ -31,11 +31,11 @@ def tile_multilatentattention_pb_v_kernel(tc, x, wd, wu, rope_cos, rope_sin, g, 
     g_view = g.rearrange("b (p j) h f -> b p j (h f)", j=4)
     x_view = x.rearrange("b (p j) d -> b p j d", j=4)
     wu_view = wu.rearrange("(p u e) f -> p u e f", u=2, e=2)
-    wd_view = wd.rearrange("(n p i) l -> p n i l", p=P, i=2)
+    wd_view = wd.rearrange("(n p i) l -> p n i l", p=P, i=4)
     cos_view = rope_cos.rearrange("(p j) r -> p j r", j=4)
     sin_view = rope_sin.rearrange("(p j) r -> p j r", j=4)
     out0_view = out_0.rearrange("b (p j) d -> b p j d", j=4)
-    out1_view = out_1.rearrange("(a p) l -> p a l", p=P)
+    out1_view = out_1.rearrange("(n h p i) l -> p n h i l", h=2, p=P, i=2)
 
     with ExitStack() as ctx:
         keep = ctx.enter_context(tc.tile_pool(name="keep", bufs=1))
@@ -58,6 +58,9 @@ def tile_multilatentattention_pb_v_kernel(tc, x, wd, wu, rope_cos, rope_sin, g, 
         x_codes = keep.tile([P, B, D], U32, align_bytes=64)
         x_scales = keep.tile([P, B, D], U8, align_bytes=64)
 
+        zeros = keep.tile([P, 512], BF16, align_bytes=64)
+        nc.vector.memset(zeros[:], 0.0)
+
         with tc.manual_schedule():
             nc.scalar.copy(out=warm2[:], in_=warm[:])
 
@@ -72,13 +75,13 @@ def tile_multilatentattention_pb_v_kernel(tc, x, wd, wu, rope_cos, rope_sin, g, 
                 return t
 
             def load_wd(c):
-                t = raw.tile([P, 4, 2, DL], BF16, name="wd_raw", tag="rawb", bufs=4, align_bytes=64)
-                nc.sync.dma_start(out=t[:], in_=wd_view[:, 4 * c : 4 * c + 4])
+                t = raw.tile([P, 4, DL], BF16, name="wd_raw", tag="rawa", align_bytes=64)
+                nc.sync.dma_start(out=t[:], in_=wd_view[:, c])
                 return t
 
-            def load_x(half, b):
-                t = raw.tile([P, 4, D // 2], BF16, name="x_raw", tag="rawb", bufs=4, align_bytes=64)
-                nc.sync.dma_start(out=t[:], in_=x_view[b][:, :, half * (D // 2) : (half + 1) * (D // 2)])
+            def load_x(b):
+                t = keep.tile([P, 4, D], BF16, name=f"x_raw{b}", align_bytes=64)
+                nc.sync.dma_start(out=t[:], in_=x_view[b])
                 return t
 
             wu_raw = {}
@@ -92,23 +95,25 @@ def tile_multilatentattention_pb_v_kernel(tc, x, wd, wu, rope_cos, rope_sin, g, 
                 nc.sync.dma_start(out=t[:], in_=g[0].rearrange("(p j) h f -> p j h f", j=4)[:, 0, half * 8 : half * 8 + 8])
                 g0_parts.append(t)
 
-            nc.sync.dma_start(out=cos_t[:], in_=cos_view)
-            nc.sync.dma_start(out=sin_t[:], in_=sin_view)
+            nc.sync.dma_start(out=cos_t[:, 0:1, :], in_=cos_view[:, 0:1, :])
+            nc.sync.dma_start(out=sin_t[:, 0:1, :], in_=sin_view[:, 0:1, :])
             wu_raw[0, 0] = load_wu(0, 0)
             load_g0(0)
             load_g0(1)
             wu_raw[1, 0] = load_wu(1, 0)
+            nc.sync.dma_start(out=cos_t[:, 1:4, :], in_=cos_view[:, 1:4, :])
+            nc.sync.dma_start(out=sin_t[:, 1:4, :], in_=sin_view[:, 1:4, :])
             g_raw[1] = load_g(1)
             wu_raw[0, 1] = load_wu(0, 1)
             wu_raw[1, 1] = load_wu(1, 1)
             for c in range(2):
                 g_raw[2 + c] = load_g(2 + c)
-                wd_raw[c] = load_wd(c)
+                wd_raw[2 * c] = load_wd(2 * c)
+                wd_raw[2 * c + 1] = load_wd(2 * c + 1)
             for k in range(4, TILES):
                 g_raw[k] = load_g(k)
-            for half in range(2):
-                for b in range(B):
-                    x_raw[half, b] = load_x(half, b)
+            for b in range(B):
+                x_raw[b] = load_x(b)
 
             def copy_out(engine, out, in_):
                 if engine == "v":
@@ -116,8 +121,11 @@ def tile_multilatentattention_pb_v_kernel(tc, x, wd, wu, rope_cos, rope_sin, g, 
                 else:
                     nc.scalar.copy(out=out, in_=in_)
 
-            def new_bank():
-                return psum.tile([P, 512], F32, name="bank", tag="bank")
+            def new_bank(warm=0):
+                bank = psum.tile([P, 512], F32, name="bank", tag="bank")
+                for i in range(warm):
+                    nc.tensor.matmul(bank[:], lhsT=zeros[:, :P], rhs=zeros[:], start=True, stop=True)
+                return bank
 
             grp = {}
             ropes = {}
@@ -140,9 +148,9 @@ def tile_multilatentattention_pb_v_kernel(tc, x, wd, wu, rope_cos, rope_sin, g, 
                     nc.vector.tensor_tensor(out=t[:, :, DH : DH + 32], in0=pc[:, :n, 0:32], in1=ps[:, :n, 32:64], op=ADD)
                     nc.vector.tensor_tensor(out=t[:, :, DH + 32 : HF], in0=pc[:, :n, 32:64], in1=ps[:, :n, 0:32], op=SUB)
 
-            def wu_bank(u, s):
+            def wu_bank(u, s, warm=0):
                 src = wu_raw[u, s // 3]
-                bank = new_bank()
+                bank = new_bank(warm)
                 for e in range(2):
                     words = src[:, e, (s % 3) * 512 : (s % 3 + 1) * 512].bitcast(F32)
                     for w in range(2):
@@ -163,27 +171,28 @@ def tile_multilatentattention_pb_v_kernel(tc, x, wd, wu, rope_cos, rope_sin, g, 
                     in_=grouped[:],
                 )
 
-            def wd_bank(n):
-                src = wd_raw[n // 4]
-                bank = new_bank()
+            wd_grp = {}
+
+            def wd_bank(n, warm=0):
+                c, half = n // 2, n % 2
+                if half == 0:
+                    wd_grp[c] = work.tile([P, 512, 4], BF16, name="wd_grp", tag="xgrp", bufs=3, align_bytes=64)
+                bank = new_bank(warm)
                 for i in range(2):
-                    words = src[:, n % 4, i, :].bitcast(F32)
+                    words = wd_raw[c][:, 2 * half + i, :].bitcast(F32)
                     for w in range(2):
                         q = 2 * i + w
                         nc.tensor.transpose(bank[:, q * P : (q + 1) * P], words[:, w:256:2], ident[:])
-                grouped = work.tile([P, 1024], BF16, name="wd_grp", tag="wgrp", bufs=3, align_bytes=64)
                 nc.scalar.copy(
-                    out=grouped[:].bitcast(F32).rearrange("p (m i w) -> p m i w", i=2, w=2),
+                    out=wd_grp[c][:].rearrange("p c t -> p (c t)").bitcast(F32).rearrange("p (m i w) -> p m i w", i=4, w=2)[:, :, 2 * half : 2 * half + 2, :],
                     in_=bank[:].rearrange("p (i w m) -> p m i w", i=2, w=2),
                 )
-                return n, grouped
 
-            def wd_quant(item):
-                n, grouped = item
+            def wd_quant(c):
                 nc.vector.quantize_mx(
-                    out=wd_codes[:, 256 * n : 256 * n + 256].bitcast(E4M3),
-                    scales=wd_scales[:, 256 * n : 256 * n + 256],
-                    in_=grouped[:],
+                    out=wd_codes[:, 512 * c : 512 * c + 512].bitcast(E4M3),
+                    scales=wd_scales[:, 512 * c : 512 * c + 512],
+                    in_=wd_grp[c][:].rearrange("p c t -> p (c t)"),
                 )
 
             def g_words(k, s):
@@ -194,10 +203,10 @@ def tile_multilatentattention_pb_v_kernel(tc, x, wd, wu, rope_cos, rope_sin, g, 
                     flat = g_raw[k][:].rearrange("p h f -> p (h f)")
                 return flat[:, 512 * s : 512 * s + 512].bitcast(F32)
 
-            def dz2_bank(k, c):
+            def dz2_bank(k, c, warm=0):
                 if c == 0:
                     grp[k] = work.tile([P, J], BF16, name="g_grp", tag="ggrp", bufs=2, align_bytes=64)
-                bank = new_bank()
+                bank = new_bank(warm)
                 for i in range(2):
                     words = g_words(k, 2 * c + i)
                     for w in range(2):
@@ -293,18 +302,14 @@ def tile_multilatentattention_pb_v_kernel(tc, x, wd, wu, rope_cos, rope_sin, g, 
             dz1 = {}
             dz1_grp = {}
 
-            def interleave(engine, dst, src):
-                out = dst.rearrange("p (c i) t -> p c t i", i=4)
-                in_ = src.rearrange("p t (c i) -> p c t i", i=4)
-                if engine == "v":
-                    nc.vector.tensor_copy(out=out, in_=in_)
-                else:
-                    nc.scalar.copy(out=out, in_=in_)
-
-            def dz1_interleave(b):
-                grouped = work.tile([P, DL, 4], BF16, name="dz1_grp", tag="xgrp", bufs=3, align_bytes=64)
-                interleave("v", grouped[:], dz1_tok[b][:])
-                dz1_grp[b] = grouped
+            def dz1_interleave(b, engine, lo, hi):
+                if lo == 0:
+                    dz1_grp[b] = work.tile([P, DL, 4], BF16, name="dz1_grp", tag="xgrp", bufs=3, align_bytes=64)
+                copy_out(
+                    engine,
+                    dz1_grp[b][:, lo:hi, :].rearrange("p (g l) t -> p g t l", l=4),
+                    dz1_tok[b][:, :, lo:hi].rearrange("p t (g l) -> p g t l", l=4),
+                )
 
             def dz1_quant(b):
                 codes = keep.tile([P, DL], U32, name=f"dz1_codes{b}", align_bytes=64)
@@ -316,9 +321,13 @@ def tile_multilatentattention_pb_v_kernel(tc, x, wd, wu, rope_cos, rope_sin, g, 
 
             x_grp = {}
 
-            def x_interleave(engine, n, b):
+            def x_interleave(n, b):
                 grouped = work.tile([P, 512, 4], BF16, name="x_grp", tag="xgrp", bufs=3, align_bytes=64)
-                interleave(engine, grouped[:], x_raw[n // 2, b][:, :, 512 * (n % 2) : 512 * (n % 2) + 512])
+                for i in range(2):
+                    nc.vector.tensor_copy(
+                        out=grouped[:, 256 * i : 256 * i + 256, :].rearrange("p (g l) t -> p g t l", l=4),
+                        in_=x_raw[b][:, :, 512 * n + i : 512 * n + 512 : 2].rearrange("p t (g l) -> p g t l", l=4),
+                    )
                 x_grp[n, b] = grouped
 
             def x_quant(n, b):
@@ -329,74 +338,78 @@ def tile_multilatentattention_pb_v_kernel(tc, x, wd, wu, rope_cos, rope_sin, g, 
                 )
 
             res1 = {}
+            acc1 = {}
 
-            def out1_tile(a, engine):
-                if a % 2 == 0:
-                    res1[a // 2] = work.tile([P, 2, DL], F32, name="res1", tag="res1", bufs=4, align_bytes=64)
-                bank = new_bank()
-                for b in range(B):
-                    codes, scales = dz1[b]
-                    nc.tensor.matmul_mx(
-                        out=bank[:],
-                        lhsT=x_codes[:, b, P * a : P * a + P].bitcast(E4M3),
-                        lhsT_scale=x_scales[:, b, P * a : P * a + P],
-                        rhs=codes[:].bitcast(E5M2),
-                        rhs_scale=scales[:],
-                        start=(b == 0),
-                        stop=(b == B - 1),
-                    )
-                res = res1[a // 2][:, a % 2, :]
-                out = res.rearrange("p (m u e) -> p m u e", u=2, e=2)
-                in_ = bank[:].rearrange("p (u m e) -> p m u e", u=2, e=2)
-                if engine == "v":
-                    nc.vector.tensor_copy(out=out, in_=in_)
-                else:
-                    nc.scalar.copy(out=out, in_=in_)
-                if a % 2 == 1:
-                    nc.sync.dma_start(out=out1_view[:, a - 1 : a + 1, :], in_=res1[a // 2][:])
+            def out1_pass(j, b):
+                n, h, i = j // 4, j // 2 % 2, j % 2
+                a = 4 * n + 2 * i + h
+                codes, scales = dz1[b]
+                if b == 0:
+                    acc1[j] = new_bank()
+                nc.tensor.matmul_mx(
+                    out=acc1[j][:],
+                    lhsT=x_codes[:, b, P * a : P * a + P].bitcast(E4M3),
+                    lhsT_scale=x_scales[:, b, P * a : P * a + P],
+                    rhs=codes[:].bitcast(E5M2),
+                    rhs_scale=scales[:],
+                    start=(b == 0),
+                    stop=(b == B - 1),
+                )
+
+            def out1_copy(j, engine):
+                n, h, i = j // 4, j // 2 % 2, j % 2
+                if i == 0:
+                    res1[j // 2] = work.tile([P, 2, DL], F32, name="res1", tag="res1", bufs=4, align_bytes=64)
+                copy_out(
+                    engine,
+                    res1[j // 2][:, i, :].rearrange("p (m u e) -> p m u e", u=2, e=2),
+                    acc1[j][:].rearrange("p (u m e) -> p m u e", u=2, e=2),
+                )
+                if i == 1:
+                    nc.sync.dma_start(out=out1_view[:, n, h], in_=res1[j // 2][:])
 
             def rope(k):
                 rope_add(rope_mul([g_raw[k]], k), k)
 
-            def dz2_step(k, cs):
+            def dz2_step(k, cs, warm=0):
                 for c in cs:
-                    dz2_copy(k, c, dz2_bank(k, c))
+                    dz2_copy(k, c, dz2_bank(k, c, warm if c == cs[0] else 0))
 
             xs = [(n, b) for n in range(4) for b in range(B)]
             pend = []
 
             def x_step():
                 xu = xs.pop(0)
-                x_interleave("v", *xu)
+                x_interleave(*xu)
                 if pend:
                     x_quant(*pend.pop())
                 pend.append(xu)
 
-            w00 = [wu_bank(0, s) for s in range(3)]
+            w00 = [wu_bank(0, s, 10 if s == 0 else 0) for s in range(3)]
             rope_add(rope_mul(g0_parts[:1], 0), 0)
             w10 = []
             for s in range(3):
                 wu_quant(w00[s])
-                w10.append(wu_bank(1, s))
-            dz2_step(0, (0,))
+                w10.append(wu_bank(1, s, 4 if s == 0 else 0))
+            dz2_step(0, (0,), 2)
             rope_add(rope_mul(g0_parts[1:], 0), 0)
             for item in w10:
                 wu_quant(item)
             dz2_step(0, (1, 2))
             rope(1)
-            w01 = [wu_bank(0, s) for s in range(3, 6)]
+            w01 = [wu_bank(0, s, 2 if s == 3 else 0) for s in range(3, 6)]
             dz2_quant(0, grp[0])
             w11 = []
             for s in range(3):
                 wu_quant(w01[s])
-                w11.append(wu_bank(1, 3 + s))
+                w11.append(wu_bank(1, 3 + s, 2 if s == 0 else 0))
             for item in w11:
                 wu_quant(item)
             ropes_at = {0: (2,), 1: (3, 4), 2: (5,), 3: (6,), 4: (7,)}
             left = None
             for k in range(TILES):
                 if k + 1 < TILES:
-                    dz2_step(k + 1, (0, 1))
+                    dz2_step(k + 1, (0, 1), 2 if k == 0 else 0)
                 if k >= 2:
                     for n in range(4):
                         out0_part(k - 2, n, "v" if n == 3 and k in (5, 7) else "s")
@@ -418,21 +431,19 @@ def tile_multilatentattention_pb_v_kernel(tc, x, wd, wu, rope_cos, rope_sin, g, 
                 if k >= 1:
                     stage1(k)
                     stage1_copy(k)
-                wds = []
                 if k < 2:
                     for n in range(4 * k, 4 * k + 4):
-                        wds.append(wd_bank(n))
-                        if len(wds) == 3:
-                            wd_quant(wds.pop(0))
+                        wd_bank(n, (2, 0, 1, 0, 0, 0, 2, 0)[n])
+                    wd_quant(2 * k)
                 if k == 0:
                     stage1(k)
                     stage1_copy(k)
                 if k + 1 < TILES:
                     dz2_quant(k + 1, grp[k + 1])
-                for item in wds:
-                    wd_quant(item)
+                if k < 2:
+                    wd_quant(2 * k + 1)
                 if k == 4:
-                    dz1_interleave(0)
+                    dz1_interleave(0, "v", 0, DL)
                 if k in (4, 6):
                     x_step()
                 if k == 4:
@@ -441,14 +452,16 @@ def tile_multilatentattention_pb_v_kernel(tc, x, wd, wu, rope_cos, rope_sin, g, 
                 out0_part(6, n, "s")
                 if n == 1:
                     dz1_transpose(7)
-            dz1_interleave(1)
+            dz1_interleave(1, "v", 0, DL)
             dz1f_quant(7)
             dz1_quant(1)
             for n in range(4):
                 out0_part(7, n, "s")
-            for a in range(16):
-                while len(xs) > 0 and xs[0][0] <= (a + 4) // 4:
+            for j in range(16):
+                while len(xs) > 0 and xs[0][0] <= (j + 4) // 4:
                     x_step()
-                if len(pend) > 0 and (pend[0][0] <= a // 4 or len(xs) == 0):
+                if len(pend) > 0 and (pend[0][0] <= j // 4 or len(xs) == 0):
                     x_quant(*pend.pop())
-                out1_tile(a, "v" if a in (11, 12, 14) else "s")
+                out1_pass(j, 0)
+                out1_pass(j, 1)
+                out1_copy(j, "v" if j in (11, 12, 14) else "s")

from contextlib import ExitStack

import concourse.mybir as mybir
from concourse.masks import make_identity

B, S, D, H, DH, DL, DR = 2, 512, 2048, 16, 128, 512, 64
T = B * S
J = H * (DH + DR)
FLOPS = 2 * T * J * DL + 2 * T * DL * D + 2 * D * T * DL

F32 = mybir.dt.float32
BF16 = mybir.dt.bfloat16
U32 = mybir.dt.uint32
U8 = mybir.dt.uint8
E4M3 = mybir.dt.float8_e4m3fn_x4
E5M2 = mybir.dt.float8_e5m2_x4
MULT = mybir.AluOpType.mult
ADD = mybir.AluOpType.add
SUB = mybir.AluOpType.subtract

P = 128
PASSES = J // 512
TILES = T // P
GTILES = S // P
HF = DH + DR


def tile_multilatentattention_pb_v_kernel(tc, x, wd, wu, rope_cos, rope_sin, g, out_0, out_1):
    nc = tc.nc

    g_view = g.rearrange("b (p j) h f -> b p j (h f)", j=4)
    x_view = x.rearrange("b (p j) d -> b p j d", j=4)
    wu_view = wu.rearrange("(p u e) f -> p u e f", u=2, e=2)
    wd_view = wd.rearrange("(n p i) l -> p n i l", p=P, i=4)
    cos_view = rope_cos.rearrange("(p j) r -> p j r", j=4)
    sin_view = rope_sin.rearrange("(p j) r -> p j r", j=4)
    out0_view = out_0.rearrange("b (p j) d -> b p j d", j=4)
    out1_view = out_1.rearrange("(n h p i) l -> p n h i l", h=2, p=P, i=2)

    with ExitStack() as ctx:
        keep = ctx.enter_context(tc.tile_pool(name="keep", bufs=1))
        raw = ctx.enter_context(tc.tile_pool(name="raw", bufs=7))
        work = ctx.enter_context(tc.tile_pool(name="work", bufs=2))
        psum = ctx.enter_context(tc.psum_pool(name="psum", bufs=8))

        ident = keep.tile([P, P], F32, align_bytes=64)
        make_identity(nc, ident[:])
        warm = keep.tile([P, 16], F32, align_bytes=64)
        nc.vector.memset(warm[:], 0.0)
        warm2 = keep.tile([P, 16], F32, align_bytes=64)

        cos_t = keep.tile([P, 4, DR], F32, align_bytes=64)
        sin_t = keep.tile([P, 4, DR], F32, align_bytes=64)
        wu_codes = keep.tile([P, PASSES, DL], U32, align_bytes=64)
        wu_scales = keep.tile([P, PASSES, DL], U8, align_bytes=64)
        wd_codes = keep.tile([P, D], U32, align_bytes=64)
        wd_scales = keep.tile([P, D], U8, align_bytes=64)
        x_codes = keep.tile([P, B, D], U32, align_bytes=64)
        x_scales = keep.tile([P, B, D], U8, align_bytes=64)

        zeros = keep.tile([P, 512], BF16, align_bytes=64)
        nc.vector.memset(zeros[:], 0.0)

        with tc.manual_schedule():
            nc.scalar.copy(out=warm2[:], in_=warm[:])

            def load_g(k):
                t = raw.tile([P, H, HF], BF16, name="g_raw", tag="rawa", align_bytes=64)
                nc.sync.dma_start(out=t[:], in_=g[k // 4].rearrange("(p j) h f -> p j h f", j=4)[:, k % 4])
                return t

            def load_wu(u, half):
                t = raw.tile([P, 2, J // 2], BF16, name="wu_raw", tag="rawa", align_bytes=64)
                nc.sync.dma_start(out=t[:], in_=wu_view[:, u, :, half * (J // 2) : (half + 1) * (J // 2)])
                return t

            def load_wd(c):
                t = raw.tile([P, 4, DL], BF16, name="wd_raw", tag="rawa", align_bytes=64)
                nc.sync.dma_start(out=t[:], in_=wd_view[:, c])
                return t

            def load_x(b):
                t = keep.tile([P, 4, D], BF16, name=f"x_raw{b}", align_bytes=64)
                nc.sync.dma_start(out=t[:], in_=x_view[b])
                return t

            wu_raw = {}
            g_raw = {}
            wd_raw = {}
            x_raw = {}
            g0_parts = []

            def load_g0(half):
                t = keep.tile([P, H // 2, HF], BF16, name=f"g0_{half}", align_bytes=64)
                nc.sync.dma_start(out=t[:], in_=g[0].rearrange("(p j) h f -> p j h f", j=4)[:, 0, half * 8 : half * 8 + 8])
                g0_parts.append(t)

            nc.sync.dma_start(out=cos_t[:, 0:1, :], in_=cos_view[:, 0:1, :])
            nc.sync.dma_start(out=sin_t[:, 0:1, :], in_=sin_view[:, 0:1, :])
            wu_raw[0, 0] = load_wu(0, 0)
            load_g0(0)
            load_g0(1)
            wu_raw[1, 0] = load_wu(1, 0)
            nc.sync.dma_start(out=cos_t[:, 1:4, :], in_=cos_view[:, 1:4, :])
            nc.sync.dma_start(out=sin_t[:, 1:4, :], in_=sin_view[:, 1:4, :])
            g_raw[1] = load_g(1)
            wu_raw[0, 1] = load_wu(0, 1)
            wu_raw[1, 1] = load_wu(1, 1)
            for c in range(2):
                g_raw[2 + c] = load_g(2 + c)
                wd_raw[2 * c] = load_wd(2 * c)
                wd_raw[2 * c + 1] = load_wd(2 * c + 1)
            for k in range(4, TILES):
                g_raw[k] = load_g(k)
            for b in range(B):
                x_raw[b] = load_x(b)

            def copy_out(engine, out, in_):
                if engine == "v":
                    nc.vector.tensor_copy(out=out, in_=in_)
                else:
                    nc.scalar.copy(out=out, in_=in_)

            def new_bank(warm=0):
                bank = psum.tile([P, 512], F32, name="bank", tag="bank")
                for i in range(warm):
                    nc.tensor.matmul(bank[:], lhsT=zeros[:, :P], rhs=zeros[:], start=True, stop=True)
                return bank

            grp = {}
            ropes = {}

            def rope_mul(parts, k):
                res = []
                for t in parts:
                    heads = t.shape[1]
                    gr = t[:, :, DH:HF]
                    pc = work.tile([P, H, DR], F32, name="pc", tag="pc", bufs=2, align_bytes=64)
                    ps = work.tile([P, H, DR], F32, name="ps", tag="ps", bufs=2, align_bytes=64)
                    shape = [P, heads, DR]
                    nc.vector.tensor_tensor(out=pc[:, :heads], in0=gr, in1=cos_t[:, k % 4, :].unsqueeze(1).to_broadcast(shape), op=MULT)
                    nc.vector.tensor_tensor(out=ps[:, :heads], in0=gr, in1=sin_t[:, k % 4, :].unsqueeze(1).to_broadcast(shape), op=MULT)
                    res.append((t, pc, ps, heads))
                return res

            def rope_add(items, k):
                for t, pc, ps, n in items:
                    nc.vector.tensor_tensor(out=t[:, :, DH : DH + 32], in0=pc[:, :n, 0:32], in1=ps[:, :n, 32:64], op=ADD)
                    nc.vector.tensor_tensor(out=t[:, :, DH + 32 : HF], in0=pc[:, :n, 32:64], in1=ps[:, :n, 0:32], op=SUB)

            def wu_bank(u, s, warm=0):
                src = wu_raw[u, s // 3]
                bank = new_bank(warm)
                for e in range(2):
                    words = src[:, e, (s % 3) * 512 : (s % 3 + 1) * 512].bitcast(F32)
                    for w in range(2):
                        q = 2 * e + w
                        nc.tensor.transpose(bank[:, q * P : (q + 1) * P], words[:, w:256:2], ident[:])
                grouped = work.tile([P, 1024], BF16, name="wu_grp", tag="wgrp", bufs=3, align_bytes=64)
                nc.scalar.copy(
                    out=grouped[:].bitcast(F32).rearrange("p (m e w) -> p m e w", e=2, w=2),
                    in_=bank[:].rearrange("p (e w m) -> p m e w", e=2, w=2),
                )
                return u, s, grouped

            def wu_quant(item):
                u, s, grouped = item
                nc.vector.quantize_mx(
                    out=wu_codes[:, s, 256 * u : 256 * u + 256].bitcast(E4M3),
                    scales=wu_scales[:, s, 256 * u : 256 * u + 256],
                    in_=grouped[:],
                )

            wd_grp = {}

            def wd_bank(n, warm=0):
                c, half = n // 2, n % 2
                if half == 0:
                    wd_grp[c] = work.tile([P, 512, 4], BF16, name="wd_grp", tag="xgrp", bufs=3, align_bytes=64)
                bank = new_bank(warm)
                for i in range(2):
                    words = wd_raw[c][:, 2 * half + i, :].bitcast(F32)
                    for w in range(2):
                        q = 2 * i + w
                        nc.tensor.transpose(bank[:, q * P : (q + 1) * P], words[:, w:256:2], ident[:])
                nc.scalar.copy(
                    out=wd_grp[c][:].rearrange("p c t -> p (c t)").bitcast(F32).rearrange("p (m i w) -> p m i w", i=4, w=2)[:, :, 2 * half : 2 * half + 2, :],
                    in_=bank[:].rearrange("p (i w m) -> p m i w", i=2, w=2),
                )

            def wd_quant(c):
                nc.vector.quantize_mx(
                    out=wd_codes[:, 512 * c : 512 * c + 512].bitcast(E4M3),
                    scales=wd_scales[:, 512 * c : 512 * c + 512],
                    in_=wd_grp[c][:].rearrange("p c t -> p (c t)"),
                )

            def g_words(k, s):
                if k == 0:
                    flat = g0_parts[s // 3][:].rearrange("p h f -> p (h f)")
                    s = s % 3
                else:
                    flat = g_raw[k][:].rearrange("p h f -> p (h f)")
                return flat[:, 512 * s : 512 * s + 512].bitcast(F32)

            def dz2_bank(k, c, warm=0):
                if c == 0:
                    grp[k] = work.tile([P, J], BF16, name="g_grp", tag="ggrp", bufs=2, align_bytes=64)
                bank = new_bank(warm)
                for i in range(2):
                    words = g_words(k, 2 * c + i)
                    for w in range(2):
                        q = 2 * i + w
                        nc.tensor.transpose(bank[:, q * P : (q + 1) * P], words[:, w:256:2], ident[:])
                return bank

            def dz2_copy(k, c, bank):
                nc.scalar.copy(
                    out=grp[k][:, 1024 * c : 1024 * c + 1024].bitcast(F32).rearrange("p (i r w) -> p i r w", i=2, w=2),
                    in_=bank[:].rearrange("p (i w r) -> p i r w", i=2, w=2),
                )

            dz2 = {}

            def dz2_quant(k, grouped):
                codes = work.tile([P, PASSES, P], U32, name="dz2_codes", tag="dz2c", bufs=3, align_bytes=64)
                scales = work.tile([P, PASSES, P], U8, name="dz2_scales", tag="dz2s", bufs=3, align_bytes=64)
                for a, b in ((0, 4), (4, 6)):
                    nc.vector.quantize_mx(
                        out=codes[:, a:b, :].rearrange("p s r -> p (s r)").bitcast(E5M2),
                        scales=scales[:, a:b, :].rearrange("p s r -> p (s r)"),
                        in_=grouped[:, 512 * a : 512 * b],
                    )
                dz2[k] = (codes, scales)

            dz1_tok = {}
            acc = {}

            def stage1(k, lo=0, hi=PASSES):
                codes, scales = dz2[k]
                if lo == 0:
                    acc[k] = new_bank()
                for s in range(lo, hi):
                    nc.tensor.matmul_mx(
                        out=acc[k][:],
                        lhsT=codes[:, s, :].bitcast(E5M2),
                        lhsT_scale=scales[:, s, :],
                        rhs=wu_codes[:, s, :].bitcast(E4M3),
                        rhs_scale=wu_scales[:, s, :],
                        start=(s == 0),
                        stop=(s == PASSES - 1),
                    )

            def stage1_copy(k):
                if k % GTILES == 0:
                    dz1_tok[k // GTILES] = work.tile([P, GTILES, DL], BF16, name="dz1_tok", tag="dz1t", bufs=2, align_bytes=64)
                nc.scalar.copy(out=dz1_tok[k // GTILES][:, k % GTILES, :], in_=acc[k][:])

            dz1f_grp = {}

            def dz1_transpose(k):
                words = dz1_tok[k // GTILES][:, k % GTILES, :].bitcast(F32)
                bank = new_bank()
                for u in range(2):
                    nc.tensor.transpose(bank[:, u * P : (u + 1) * P], words[:, u * P : (u + 1) * P], ident[:])
                grouped = work.tile([P, DL], BF16, name="dz1f_grp", tag="dz1fg", bufs=2, align_bytes=64)
                nc.scalar.copy(
                    out=grouped[:].bitcast(F32).rearrange("p (r u) -> p r u", u=2),
                    in_=bank[:, : 2 * P].rearrange("p (u r) -> p r u", u=2),
                )
                dz1f_grp[k] = grouped

            dz1f = {}

            def dz1f_quant(k):
                codes = work.tile([P, P], U32, name="dz1f_codes", tag="dz1fc", bufs=3, align_bytes=64)
                scales = work.tile([P, P], U8, name="dz1f_scales", tag="dz1fs", bufs=3, align_bytes=64)
                nc.vector.quantize_mx(out=codes[:].bitcast(E5M2), scales=scales[:], in_=dz1f_grp[k][:])
                dz1f[k] = (codes, scales)

            res0 = {}

            def out0_part(k, n, engine):
                codes, scales = dz1f[k]
                if n == 0:
                    res0[k] = work.tile([P, D], F32, name="res0", tag="res0", bufs=2, align_bytes=64)
                bank = new_bank()
                nc.tensor.matmul_mx(
                    out=bank[:],
                    lhsT=codes[:].bitcast(E5M2),
                    lhsT_scale=scales[:],
                    rhs=wd_codes[:, 512 * n : 512 * n + 512].bitcast(E4M3),
                    rhs_scale=wd_scales[:, 512 * n : 512 * n + 512],
                    start=True,
                    stop=True,
                )
                copy_out(engine, res0[k][:, 512 * n : 512 * n + 512], bank[:])
                if n % 2 == 1:
                    lo = 1024 * (n // 2)
                    nc.sync.dma_start(out=out0_view[k // GTILES][:, k % GTILES, lo : lo + 1024], in_=res0[k][:, lo : lo + 1024])

            dz1 = {}
            dz1_grp = {}

            def dz1_interleave(b, engine, lo, hi):
                if lo == 0:
                    dz1_grp[b] = work.tile([P, DL, 4], BF16, name="dz1_grp", tag="xgrp", bufs=3, align_bytes=64)
                copy_out(
                    engine,
                    dz1_grp[b][:, lo:hi, :].rearrange("p (g l) t -> p g t l", l=4),
                    dz1_tok[b][:, :, lo:hi].rearrange("p t (g l) -> p g t l", l=4),
                )

            def dz1_quant(b):
                codes = keep.tile([P, DL], U32, name=f"dz1_codes{b}", align_bytes=64)
                scales = keep.tile([P, DL], U8, name=f"dz1_scales{b}", align_bytes=64)
                nc.vector.quantize_mx(
                    out=codes[:].bitcast(E5M2), scales=scales[:], in_=dz1_grp[b][:].rearrange("p c t -> p (c t)")
                )
                dz1[b] = (codes, scales)

            x_grp = {}

            def x_interleave(n, b):
                grouped = work.tile([P, 512, 4], BF16, name="x_grp", tag="xgrp", bufs=3, align_bytes=64)
                for i in range(2):
                    nc.vector.tensor_copy(
                        out=grouped[:, 256 * i : 256 * i + 256, :].rearrange("p (g l) t -> p g t l", l=4),
                        in_=x_raw[b][:, :, 512 * n + i : 512 * n + 512 : 2].rearrange("p t (g l) -> p g t l", l=4),
                    )
                x_grp[n, b] = grouped

            def x_quant(n, b):
                nc.vector.quantize_mx(
                    out=x_codes[:, b, 512 * n : 512 * n + 512].bitcast(E4M3),
                    scales=x_scales[:, b, 512 * n : 512 * n + 512],
                    in_=x_grp[n, b][:].rearrange("p c t -> p (c t)"),
                )

            res1 = {}
            acc1 = {}

            def out1_pass(j, b):
                n, h, i = j // 4, j // 2 % 2, j % 2
                a = 4 * n + 2 * i + h
                codes, scales = dz1[b]
                if b == 0:
                    acc1[j] = new_bank()
                nc.tensor.matmul_mx(
                    out=acc1[j][:],
                    lhsT=x_codes[:, b, P * a : P * a + P].bitcast(E4M3),
                    lhsT_scale=x_scales[:, b, P * a : P * a + P],
                    rhs=codes[:].bitcast(E5M2),
                    rhs_scale=scales[:],
                    start=(b == 0),
                    stop=(b == B - 1),
                )

            def out1_copy(j, engine):
                n, h, i = j // 4, j // 2 % 2, j % 2
                if i == 0:
                    res1[j // 2] = work.tile([P, 2, DL], F32, name="res1", tag="res1", bufs=4, align_bytes=64)
                copy_out(
                    engine,
                    res1[j // 2][:, i, :].rearrange("p (m u e) -> p m u e", u=2, e=2),
                    acc1[j][:].rearrange("p (u m e) -> p m u e", u=2, e=2),
                )
                if i == 1:
                    nc.sync.dma_start(out=out1_view[:, n, h], in_=res1[j // 2][:])

            def rope(k):
                rope_add(rope_mul([g_raw[k]], k), k)

            def dz2_step(k, cs, warm=0):
                for c in cs:
                    dz2_copy(k, c, dz2_bank(k, c, warm if c == cs[0] else 0))

            xs = [(n, b) for n in range(4) for b in range(B)]
            pend = []

            def x_step():
                xu = xs.pop(0)
                x_interleave(*xu)
                if pend:
                    x_quant(*pend.pop())
                pend.append(xu)

            w00 = [wu_bank(0, s, 10 if s == 0 else 0) for s in range(3)]
            rope_add(rope_mul(g0_parts[:1], 0), 0)
            w10 = []
            for s in range(3):
                wu_quant(w00[s])
                w10.append(wu_bank(1, s, 4 if s == 0 else 0))
            dz2_step(0, (0,), 2)
            rope_add(rope_mul(g0_parts[1:], 0), 0)
            for item in w10:
                wu_quant(item)
            dz2_step(0, (1, 2))
            rope(1)
            w01 = [wu_bank(0, s, 2 if s == 3 else 0) for s in range(3, 6)]
            dz2_quant(0, grp[0])
            w11 = []
            for s in range(3):
                wu_quant(w01[s])
                w11.append(wu_bank(1, 3 + s, 2 if s == 0 else 0))
            for item in w11:
                wu_quant(item)
            ropes_at = {0: (2,), 1: (3, 4), 2: (5,), 3: (6,), 4: (7,)}
            left = None
            for k in range(TILES):
                if k + 1 < TILES:
                    dz2_step(k + 1, (0, 1), 2 if k == 0 else 0)
                if k >= 2:
                    for n in range(4):
                        out0_part(k - 2, n, "v" if n == 3 and k in (5, 7) else "s")
                if k + 1 < TILES:
                    bank = dz2_bank(k + 1, 2)
                if k >= 1:
                    dz1_transpose(k - 1)
                if k + 1 < TILES:
                    dz2_copy(k + 1, 2, bank)
                for j in ropes_at.get(k, ())[:1]:
                    rope(j)
                if k == 6:
                    x_step()
                    x_step()
                if k >= 1:
                    dz1f_quant(k - 1)
                for j in ropes_at.get(k, ())[1:]:
                    rope(j)
                if k >= 1:
                    stage1(k)
                    stage1_copy(k)
                if k < 2:
                    for n in range(4 * k, 4 * k + 4):
                        wd_bank(n, (2, 0, 1, 0, 0, 0, 2, 0)[n])
                    wd_quant(2 * k)
                if k == 0:
                    stage1(k)
                    stage1_copy(k)
                if k + 1 < TILES:
                    dz2_quant(k + 1, grp[k + 1])
                if k < 2:
                    wd_quant(2 * k + 1)
                if k == 4:
                    dz1_interleave(0, "v", 0, DL)
                if k in (4, 6):
                    x_step()
                if k == 4:
                    dz1_quant(0)
            for n in range(4):
                out0_part(6, n, "s")
                if n == 1:
                    dz1_transpose(7)
            dz1_interleave(1, "v", 0, DL)
            dz1f_quant(7)
            dz1_quant(1)
            for n in range(4):
                out0_part(7, n, "s")
            for j in range(16):
                while len(xs) > 0 and xs[0][0] <= (j + 4) // 4:
                    x_step()
                if len(pend) > 0 and (pend[0][0] <= j // 4 or len(xs) == 0):
                    x_quant(*pend.pop())
                out1_pass(j, 0)
                out1_pass(j, 1)
                out1_copy(j, "v" if j in (11, 12, 14) else "s")
